import numpy as np
import ml_dtypes


def mxq(x, axis, fmt="e4m3"):
    dtype, down = {"e4m3": (ml_dtypes.float8_e4m3fn, 7), "e5m2": (ml_dtypes.float8_e5m2, 14)}[fmt]
    v = np.moveaxis(np.asarray(x, np.float32).astype(ml_dtypes.bfloat16).astype(np.float64), axis, -1)
    blocks = v.reshape(v.shape[:-1] + (-1, 32))
    amax = np.abs(blocks).max(-1, keepdims=True)
    byte = np.maximum(np.where(amax > 0, np.frexp(amax)[1] - 1 + 127, 0) - down, 1)
    scale = np.exp2(byte - 127.0)
    codes = (blocks / scale).astype(np.float32).astype(dtype).astype(np.float64)
    return np.moveaxis((codes * scale).reshape(v.shape), -1, axis)


WIDE = False


def mx_kscale(k):
    if not WIDE:
        return np.ones(k)
    levels = np.array([10, -10, 5, -5, 0])
    a = np.random.permutation(np.resize(levels, k // 512 * 4)).reshape(k // 512, 4)
    idx = np.arange(k)
    return np.exp2(a[idx // 512, idx % 128 // 32])


BF16 = ml_dtypes.bfloat16


def bf(x):
    return np.asarray(x, np.float32).astype(BF16)


def f64(x):
    return np.asarray(x).astype(np.float64)


M, SP, H, FF, NH = 512, 384, 1024, 2560, 8
EPS = 1.1920929e-07


def rms_norm(x, w):
    var = np.mean(np.square(x), axis=-1, keepdims=True)
    return x * (1.0 / np.sqrt(var + EPS)) * w


def setup_inputs():
    s = mx_kscale(H)
    return {"x": bf(np.random.standard_normal((M, H))),
            "W_qkv": bf(np.random.standard_normal((2, H, 3 * H)) * 1.25 / np.sqrt(H) / s[None, :, None]),
            "ln1": bf((1.0 + 0.1 * np.random.standard_normal((2, H))) * s)}


def reference(x, W_qkv, ln1):
    x, W_qkv, ln1 = f64(x), f64(W_qkv), f64(ln1)
    h0 = rms_norm(x[:SP], ln1[0])
    h1 = rms_norm(x[SP:], ln1[1])
    y0 = mxq(h0, 1, "e4m3") @ mxq(W_qkv[0], 0, "e4m3")
    y1 = mxq(h1, 1, "e4m3") @ mxq(W_qkv[1], 0, "e4m3")
    return np.concatenate([y0, y1], axis=0)

@@ -1,0 +1,174 @@
+from contextlib import ExitStack
+
+import concourse.mybir as mybir
+from concourse.masks import make_identity
+
+F32 = mybir.dt.float32
+BF16 = mybir.dt.bfloat16
+U32 = mybir.dt.uint32
+U8 = mybir.dt.uint8
+FP8X4 = mybir.dt.float8_e4m3fn_x4
+ALU = mybir.AluOpType
+ACT = mybir.ActivationFunctionType
+
+P = 128
+PACK = 4
+K_PASS = P * PACK
+ROWS, SPLIT, H, N_OUT = 512, 384, 1024, 3072
+EPS = 1.1920929e-07
+MODELS = 2
+PASSES = H // K_PASS
+K_BLOCKS = H // P
+ROW_TILES = ROWS // P
+FIRST_ROW_TILE = (0, SPLIT // P)
+N_ROW_TILES = (SPLIT // P, (ROWS - SPLIT) // P)
+BANK = 512
+CHUNK = 1024
+UNITS = N_OUT // CHUNK
+VECTOR_COLS = (768, 576)
+
+FLOPS = 2 * ROWS * H * N_OUT
+
+
+def tile_twomodelblockrouted_pa_kernel(tc, x, W_qkv, ln1, out):
+    nc = tc.nc
+    with ExitStack() as ctx:
+        consts = ctx.enter_context(tc.tile_pool(name="consts", bufs=1))
+        rows_pool = ctx.enter_context(tc.tile_pool(name="rows", bufs=ROW_TILES))
+        small = ctx.enter_context(tc.tile_pool(name="small", bufs=ROW_TILES))
+        weights = ctx.enter_context(tc.tile_pool(name="weights", bufs=MODELS * UNITS * PASSES))
+        grouped_pool = ctx.enter_context(tc.tile_pool(name="grouped", bufs=3))
+        quantised = ctx.enter_context(tc.tile_pool(name="quantised", bufs=4))
+        results = ctx.enter_context(tc.tile_pool(name="results", bufs=UNITS))
+
+        gain_rows = consts.tile([P, MODELS * H], BF16)
+        nc.vector.memset(gain_rows[:], 0.0)
+        ones = consts.tile([P, P], BF16)
+        nc.vector.memset(ones[:], 1.0)
+        eps = consts.tile([P, 1], F32)
+        nc.vector.memset(eps[:], EPS)
+        identity = consts.tile([P, P], BF16)
+        make_identity(nc, identity[:])
+        warm = consts.tile([P, 1], F32)
+        nc.scalar.activation(out=warm[:], in_=eps[:], func=ACT.Sqrt)
+
+        nc.scalar.dma_start(out=gain_rows[0:1, :], in_=ln1.rearrange("(o g) k -> o (g k)", o=1))
+        x_rows = []
+        for m in range(ROW_TILES):
+            x_m = rows_pool.tile([P, H], BF16, name="x_rows")
+            nc.sync.dma_start(out=x_m[:], in_=x[m * P : (m + 1) * P, :])
+            x_rows.append(x_m)
+        w_raw = {}
+        for g in range(MODELS):
+            for u in range(UNITS):
+                for c in range(PASSES):
+                    raw = weights.tile([P, PACK, CHUNK], BF16, name="w_raw")
+                    nc.sync.dma_start(
+                        out=raw[:],
+                        in_=W_qkv[
+                            g, c * K_PASS : (c + 1) * K_PASS, u * CHUNK : (u + 1) * CHUNK
+                        ].rearrange("(t p) n -> p t n", p=P),
+                    )
+                    w_raw[(g, u, c)] = raw
+
+        h_grouped = consts.tile([P, ROW_TILES, PASSES, P, PACK], BF16, align_bytes=64)
+        h_codes = consts.tile([P, ROW_TILES, PASSES, P], U32, align_bytes=64)
+        h_scales = consts.tile([P, ROW_TILES, PASSES, P], U8, align_bytes=64)
+        with tc.psum_pool(name="head_psum", bufs=4) as head_psum:
+            gains = []
+            for s in range(MODELS * PASSES):
+                gains_s = head_psum.tile([P, BANK], F32, name="gains")
+                nc.tensor.matmul(
+                    out=gains_s[:],
+                    lhsT=ones[:],
+                    rhs=gain_rows[:, s * BANK : (s + 1) * BANK],
+                    start=True,
+                    stop=True,
+                )
+                gains.append(gains_s)
+            for m in range(ROW_TILES):
+                g = 0 if m < FIRST_ROW_TILE[1] else 1
+                squares = rows_pool.tile([P, H], BF16, name="squares")
+                sum_sq = small.tile([P, 1], F32, name="sum_sq")
+                nc.scalar.activation(
+                    out=squares[:], in_=x_rows[m][:], func=ACT.Square, accum_out=sum_sq[:]
+                )
+                rms = small.tile([P, 1], F32, name="rms")
+                nc.scalar.activation(
+                    out=rms[:], in_=sum_sq[:], func=ACT.Sqrt, scale=1.0 / H, bias=eps[:]
+                )
+                rstd = small.tile([P, 1], F32, name="rstd")
+                nc.vector.reciprocal(out=rstd[:], in_=rms[:])
+                h_m = rows_pool.tile([P, H], BF16, name="h_rows")
+                for c in range(PASSES):
+                    nc.vector.scalar_tensor_tensor(
+                        out=h_m[:, c * K_PASS : (c + 1) * K_PASS],
+                        in0=x_rows[m][:, c * K_PASS : (c + 1) * K_PASS],
+                        scalar=rstd[:],
+                        in1=gains[g * PASSES + c][:],
+                        op0=ALU.mult,
+                        op1=ALU.mult,
+                    )
+                h_t = head_psum.tile([P, K_BLOCKS, P], BF16, name="h_t")
+                for b in range(K_BLOCKS):
+                    nc.tensor.transpose(h_t[:, b, :], h_m[:, b * P : (b + 1) * P], identity[:])
+                nc.scalar.copy(
+                    out=h_grouped[:, m],
+                    in_=h_t[:].rearrange("p (c t) r -> p c r t", t=PACK),
+                )
+                nc.vector.quantize_mx(
+                    out=h_codes[:, m].rearrange("p c r -> p (c r)").bitcast(FP8X4),
+                    scales=h_scales[:, m].rearrange("p c r -> p (c r)"),
+                    in_=h_grouped[:, m].rearrange("p c r t -> p (c r t)"),
+                )
+
+        acc_psum = ctx.enter_context(tc.psum_pool(name="acc_psum", bufs=8))
+        for g in range(MODELS):
+            split = VECTOR_COLS[g]
+            for u in range(UNITS):
+                w_codes = []
+                w_scales = []
+                for c in range(PASSES):
+                    raw = w_raw[(g, u, c)]
+                    grouped = grouped_pool.tile([P, CHUNK, PACK], BF16, name="w_grouped", align_bytes=64)
+                    nc.vector.tensor_copy(
+                        out=grouped[:, 0:split, :].rearrange("p (w i) t -> p w t i", i=4),
+                        in_=raw[:, :, 0:split].rearrange("p t (w i) -> p w t i", i=4),
+                    )
+                    nc.scalar.copy(
+                        out=grouped[:, split:CHUNK, :].rearrange("p (w i) t -> p w t i", i=4),
+                        in_=raw[:, :, split:CHUNK].rearrange("p t (w i) -> p w t i", i=4),
+                    )
+                    codes = quantised.tile([P, CHUNK], U32, name="w_codes", align_bytes=64)
+                    scales = quantised.tile([P, CHUNK], U8, name="w_scales", align_bytes=64)
+                    nc.vector.quantize_mx(
+                        out=codes[:].bitcast(FP8X4),
+                        scales=scales[:],
+                        in_=grouped[:].rearrange("p w t -> p (w t)"),
+                    )
+                    w_codes.append(codes)
+                    w_scales.append(scales)
+                out_rows = results.tile([P, N_ROW_TILES[g], CHUNK], F32, name="out_rows%d" % g)
+                for n in range(CHUNK // BANK):
+                    n_cols = slice(n * BANK, (n + 1) * BANK)
+                    for i in range(N_ROW_TILES[g]):
+                        m = FIRST_ROW_TILE[g] + i
+                        acc = acc_psum.tile([P, BANK], F32, name="acc")
+                        for c in range(PASSES):
+                            nc.tensor.matmul_mx(
+                                out=acc[:],
+                                lhsT=h_codes[:, m, c, :].bitcast(FP8X4),
+                                lhsT_scale=h_scales[:, m, c, :],
+                                rhs=w_codes[c][:, n_cols].bitcast(FP8X4),
+                                rhs_scale=w_scales[c][:, n_cols],
+                                start=(c == 0),
+                                stop=(c == PASSES - 1),
+                            )
+                        nc.scalar.copy(out=out_rows[:, i, n_cols], in_=acc[:])
+                first_row = FIRST_ROW_TILE[g] * P
+                nc.sync.dma_start(
+                    out=out[
+                        first_row : first_row + N_ROW_TILES[g] * P, u * CHUNK : (u + 1) * CHUNK
+                    ].rearrange("(i p) n -> p i n", p=P),
+                    in_=out_rows[:],
+                )

@@ -52,7 +52,7 @@ def tile_twomodelblockrouted_pa_kernel(tc, x, W_qkv, ln1, out):
         warm = consts.tile([P, 1], F32)
         nc.scalar.activation(out=warm[:], in_=eps[:], func=ACT.Sqrt)
 
-        nc.scalar.dma_start(out=gain_rows[0:1, :], in_=ln1.rearrange("(o g) k -> o (g k)", o=1))
+        nc.sync.dma_start(out=gain_rows[0:1, :], in_=ln1.rearrange("(o g) k -> o (g k)", o=1))
         x_rows = []
         for m in range(ROW_TILES):
             x_m = rows_pool.tile([P, H], BF16, name="x_rows")

@@ -5,6 +5,7 @@ from concourse.masks import make_identity
 
 F32 = mybir.dt.float32
 BF16 = mybir.dt.bfloat16
+I32 = mybir.dt.int32
 U32 = mybir.dt.uint32
 U8 = mybir.dt.uint8
 FP8X4 = mybir.dt.float8_e4m3fn_x4
@@ -25,7 +26,10 @@ N_ROW_TILES = (SPLIT // P, (ROWS - SPLIT) // P)
 BANK = 512
 CHUNK = 1024
 UNITS = N_OUT // CHUNK
-VECTOR_COLS = (768, 576)
+N_CHUNKS = MODELS * PASSES * UNITS
+BANKS_PER_CHUNK = CHUNK // BANK
+BASE_COLS = 624
+COLS_PER_BANK = 56
 
 FLOPS = 2 * ROWS * H * N_OUT
 
@@ -33,43 +37,44 @@ FLOPS = 2 * ROWS * H * N_OUT
 def tile_twomodelblockrouted_pa_kernel(tc, x, W_qkv, ln1, out):
     nc = tc.nc
     with ExitStack() as ctx:
+        ctx.enter_context(tc.manual_schedule())
         consts = ctx.enter_context(tc.tile_pool(name="consts", bufs=1))
-        rows_pool = ctx.enter_context(tc.tile_pool(name="rows", bufs=ROW_TILES))
+        rows_pool = ctx.enter_context(tc.tile_pool(name="rows", bufs=2))
         small = ctx.enter_context(tc.tile_pool(name="small", bufs=ROW_TILES))
-        weights = ctx.enter_context(tc.tile_pool(name="weights", bufs=MODELS * UNITS * PASSES))
+        weights = ctx.enter_context(tc.tile_pool(name="weights", bufs=MODELS * PASSES))
         grouped_pool = ctx.enter_context(tc.tile_pool(name="grouped", bufs=3))
-        quantised = ctx.enter_context(tc.tile_pool(name="quantised", bufs=4))
+        quantised = ctx.enter_context(tc.tile_pool(name="quantised", bufs=6))
         results = ctx.enter_context(tc.tile_pool(name="results", bufs=UNITS))
 
         gain_rows = consts.tile([P, MODELS * H], BF16)
-        nc.vector.memset(gain_rows[:], 0.0)
-        ones = consts.tile([P, P], BF16)
-        nc.vector.memset(ones[:], 1.0)
+        nc.vector.memset(gain_rows[:].bitcast(I32), 0)
         eps = consts.tile([P, 1], F32)
         nc.vector.memset(eps[:], EPS)
+        ones = consts.tile([P, P], BF16)
+        nc.vector.memset(ones[:], 1.0)
         identity = consts.tile([P, P], BF16)
         make_identity(nc, identity[:])
         warm = consts.tile([P, 1], F32)
         nc.scalar.activation(out=warm[:], in_=eps[:], func=ACT.Sqrt)
 
-        nc.sync.dma_start(out=gain_rows[0:1, :], in_=ln1.rearrange("(o g) k -> o (g k)", o=1))
         x_rows = []
         for m in range(ROW_TILES):
-            x_m = rows_pool.tile([P, H], BF16, name="x_rows")
+            x_m = rows_pool.tile([P, H], BF16, name="x_rows", bufs=ROW_TILES)
             nc.sync.dma_start(out=x_m[:], in_=x[m * P : (m + 1) * P, :])
             x_rows.append(x_m)
-        w_raw = {}
+            if m == 0:
+                nc.sync.dma_start(
+                    out=gain_rows[0:1, :], in_=ln1.rearrange("(o g) k -> o (g k)", o=1)
+                )
+        w_raw = []
         for g in range(MODELS):
-            for u in range(UNITS):
-                for c in range(PASSES):
-                    raw = weights.tile([P, PACK, CHUNK], BF16, name="w_raw")
-                    nc.sync.dma_start(
-                        out=raw[:],
-                        in_=W_qkv[
-                            g, c * K_PASS : (c + 1) * K_PASS, u * CHUNK : (u + 1) * CHUNK
-                        ].rearrange("(t p) n -> p t n", p=P),
-                    )
-                    w_raw[(g, u, c)] = raw
+            for c in range(PASSES):
+                raw = weights.tile([P, PACK, N_OUT], BF16, name="w_raw")
+                nc.sync.dma_start(
+                    out=raw[:],
+                    in_=W_qkv[g, c * K_PASS : (c + 1) * K_PASS, :].rearrange("(t p) n -> p t n", p=P),
+                )
+                w_raw.append(raw)
 
         h_grouped = consts.tile([P, ROW_TILES, PASSES, P, PACK], BF16, align_bytes=64)
         h_codes = consts.tile([P, ROW_TILES, PASSES, P], U32, align_bytes=64)
@@ -86,16 +91,21 @@ def tile_twomodelblockrouted_pa_kernel(tc, x, W_qkv, ln1, out):
                     stop=True,
                 )
                 gains.append(gains_s)
-            for m in range(ROW_TILES):
-                g = 0 if m < FIRST_ROW_TILE[1] else 1
+            sum_sq = []
+            h_t = []
+
+            def sum_squares(m):
                 squares = rows_pool.tile([P, H], BF16, name="squares")
-                sum_sq = small.tile([P, 1], F32, name="sum_sq")
+                sum_sq.append(small.tile([P, 1], F32, name="sum_sq"))
                 nc.scalar.activation(
-                    out=squares[:], in_=x_rows[m][:], func=ACT.Square, accum_out=sum_sq[:]
+                    out=squares[:], in_=x_rows[m][:], func=ACT.Square, accum_out=sum_sq[m][:]
                 )
+
+            def normalise_and_transpose(m):
+                g = 0 if m < FIRST_ROW_TILE[1] else 1
                 rms = small.tile([P, 1], F32, name="rms")
                 nc.scalar.activation(
-                    out=rms[:], in_=sum_sq[:], func=ACT.Sqrt, scale=1.0 / H, bias=eps[:]
+                    out=rms[:], in_=sum_sq[m][:], func=ACT.Sqrt, scale=1.0 / H, bias=eps[:]
                 )
                 rstd = small.tile([P, 1], F32, name="rstd")
                 nc.vector.reciprocal(out=rstd[:], in_=rms[:])
@@ -109,66 +119,107 @@ def tile_twomodelblockrouted_pa_kernel(tc, x, W_qkv, ln1, out):
                         op0=ALU.mult,
                         op1=ALU.mult,
                     )
-                h_t = head_psum.tile([P, K_BLOCKS, P], BF16, name="h_t")
+                h_t.append(head_psum.tile([P, K_BLOCKS, P], BF16, name="h_t"))
                 for b in range(K_BLOCKS):
-                    nc.tensor.transpose(h_t[:, b, :], h_m[:, b * P : (b + 1) * P], identity[:])
+                    nc.tensor.transpose(h_t[m][:, b, :], h_m[:, b * P : (b + 1) * P], identity[:])
+
+            sum_squares(0)
+            for m in range(1, ROW_TILES):
+                sum_squares(m)
+                normalise_and_transpose(m - 1)
+            normalise_and_transpose(ROW_TILES - 1)
+            for m in range(ROW_TILES):
                 nc.scalar.copy(
                     out=h_grouped[:, m],
-                    in_=h_t[:].rearrange("p (c t) r -> p c r t", t=PACK),
-                )
-                nc.vector.quantize_mx(
-                    out=h_codes[:, m].rearrange("p c r -> p (c r)").bitcast(FP8X4),
-                    scales=h_scales[:, m].rearrange("p c r -> p (c r)"),
-                    in_=h_grouped[:, m].rearrange("p c r t -> p (c r t)"),
+                    in_=h_t[m][:].rearrange("p (c t) r -> p c r t", t=PACK),
                 )
 
         acc_psum = ctx.enter_context(tc.psum_pool(name="acc_psum", bufs=8))
-        for g in range(MODELS):
-            split = VECTOR_COLS[g]
-            for u in range(UNITS):
-                w_codes = []
-                w_scales = []
-                for c in range(PASSES):
-                    raw = w_raw[(g, u, c)]
-                    grouped = grouped_pool.tile([P, CHUNK, PACK], BF16, name="w_grouped", align_bytes=64)
-                    nc.vector.tensor_copy(
-                        out=grouped[:, 0:split, :].rearrange("p (w i) t -> p w t i", i=4),
-                        in_=raw[:, :, 0:split].rearrange("p t (w i) -> p w t i", i=4),
-                    )
-                    nc.scalar.copy(
-                        out=grouped[:, split:CHUNK, :].rearrange("p (w i) t -> p w t i", i=4),
-                        in_=raw[:, :, split:CHUNK].rearrange("p t (w i) -> p w t i", i=4),
-                    )
-                    codes = quantised.tile([P, CHUNK], U32, name="w_codes", align_bytes=64)
-                    scales = quantised.tile([P, CHUNK], U8, name="w_scales", align_bytes=64)
-                    nc.vector.quantize_mx(
-                        out=codes[:].bitcast(FP8X4),
-                        scales=scales[:],
-                        in_=grouped[:].rearrange("p w t -> p (w t)"),
-                    )
-                    w_codes.append(codes)
-                    w_scales.append(scales)
-                out_rows = results.tile([P, N_ROW_TILES[g], CHUNK], F32, name="out_rows%d" % g)
-                for n in range(CHUNK // BANK):
-                    n_cols = slice(n * BANK, (n + 1) * BANK)
-                    for i in range(N_ROW_TILES[g]):
-                        m = FIRST_ROW_TILE[g] + i
-                        acc = acc_psum.tile([P, BANK], F32, name="acc")
-                        for c in range(PASSES):
-                            nc.tensor.matmul_mx(
-                                out=acc[:],
-                                lhsT=h_codes[:, m, c, :].bitcast(FP8X4),
-                                lhsT_scale=h_scales[:, m, c, :],
-                                rhs=w_codes[c][:, n_cols].bitcast(FP8X4),
-                                rhs_scale=w_scales[c][:, n_cols],
-                                start=(c == 0),
-                                stop=(c == PASSES - 1),
-                            )
-                        nc.scalar.copy(out=out_rows[:, i, n_cols], in_=acc[:])
-                first_row = FIRST_ROW_TILE[g] * P
-                nc.sync.dma_start(
-                    out=out[
-                        first_row : first_row + N_ROW_TILES[g] * P, u * CHUNK : (u + 1) * CHUNK
-                    ].rearrange("(i p) n -> p i n", p=P),
-                    in_=out_rows[:],
+        w_grouped = {}
+        w_codes = {}
+        w_scales = {}
+        acc = {}
+
+        def completes_columns(i):
+            return 0 <= i < N_CHUNKS and (i // UNITS) % PASSES == PASSES - 1
+
+        def banks_of(i):
+            return BANKS_PER_CHUNK * N_ROW_TILES[i // (PASSES * UNITS)] if completes_columns(i) else 0
+
+        def regroup(i, vector_cols):
+            raw = w_raw[i // UNITS]
+            first = (i % UNITS) * CHUNK
+            grouped = grouped_pool.tile([P, CHUNK, PACK], BF16, name="w_grouped", align_bytes=64)
+            nc.vector.tensor_copy(
+                out=grouped[:, 0:vector_cols, :].rearrange("p (w i) t -> p w t i", i=4),
+                in_=raw[:, :, first : first + vector_cols].rearrange("p t (w i) -> p w t i", i=4),
+            )
+            if vector_cols < CHUNK:
+                nc.scalar.copy(
+                    out=grouped[:, vector_cols:CHUNK, :].rearrange("p (w i) t -> p w t i", i=4),
+                    in_=raw[:, :, first + vector_cols : first + CHUNK].rearrange(
+                        "p t (w i) -> p w t i", i=4
+                    ),
                 )
+            w_grouped[i] = grouped
+
+        def quantise(i):
+            w_codes[i] = quantised.tile([P, CHUNK], U32, name="w_codes", align_bytes=64)
+            w_scales[i] = quantised.tile([P, CHUNK], U8, name="w_scales", align_bytes=64)
+            nc.vector.quantize_mx(
+                out=w_codes[i][:].bitcast(FP8X4),
+                scales=w_scales[i][:],
+                in_=w_grouped[i][:].rearrange("p w t -> p (w t)"),
+            )
+
+        def multiply(i):
+            g = i // (PASSES * UNITS)
+            for n in range(BANKS_PER_CHUNK):
+                n_cols = slice(n * BANK, (n + 1) * BANK)
+                for r in range(N_ROW_TILES[g]):
+                    m = FIRST_ROW_TILE[g] + r
+                    acc[(i, n, r)] = acc_psum.tile([P, BANK], F32, name="acc")
+                    for c in range(PASSES):
+                        chunk = i - (PASSES - 1 - c) * UNITS
+                        nc.tensor.matmul_mx(
+                            out=acc[(i, n, r)][:],
+                            lhsT=h_codes[:, m, c, :].bitcast(FP8X4),
+                            lhsT_scale=h_scales[:, m, c, :],
+                            rhs=w_codes[chunk][:, n_cols].bitcast(FP8X4),
+                            rhs_scale=w_scales[chunk][:, n_cols],
+                            start=(c == 0),
+                            stop=(c == PASSES - 1),
+                        )
+
+        def empty_and_store(i):
+            g, u = i // (PASSES * UNITS), i % UNITS
+            out_rows = results.tile([P, N_ROW_TILES[g], CHUNK], F32, name="out_rows%d" % g)
+            for n in range(BANKS_PER_CHUNK):
+                for r in range(N_ROW_TILES[g]):
+                    nc.scalar.copy(
+                        out=out_rows[:, r, n * BANK : (n + 1) * BANK], in_=acc[(i, n, r)][:]
+                    )
+            first_row = FIRST_ROW_TILE[g] * P
+            nc.sync.dma_start(
+                out=out[
+                    first_row : first_row + N_ROW_TILES[g] * P, u * CHUNK : (u + 1) * CHUNK
+                ].rearrange("(r p) n -> p r n", p=P),
+                in_=out_rows[:],
+            )
+
+        for s in range(N_CHUNKS + 3):
+            if s < N_CHUNKS:
+                regroup(s, min(CHUNK, BASE_COLS + COLS_PER_BANK * banks_of(s - 3)))
+            if s == 1:
+                for m in range(ROW_TILES):
+                    nc.vector.quantize_mx(
+                        out=h_codes[:, m].rearrange("p c r -> p (c r)").bitcast(FP8X4),
+                        scales=h_scales[:, m].rearrange("p c r -> p (c r)"),
+                        in_=h_grouped[:, m].rearrange("p c r t -> p (c r t)"),
+                    )
+            if 0 <= s - 1 < N_CHUNKS:
+                quantise(s - 1)
+            if completes_columns(s - 3):
+                empty_and_store(s - 3)
+            if completes_columns(s - 2):
+                multiply(s - 2)

from contextlib import ExitStack

import concourse.mybir as mybir
from concourse.masks import make_identity

F32 = mybir.dt.float32
BF16 = mybir.dt.bfloat16
I32 = mybir.dt.int32
U32 = mybir.dt.uint32
U8 = mybir.dt.uint8
FP8X4 = mybir.dt.float8_e4m3fn_x4
ALU = mybir.AluOpType
ACT = mybir.ActivationFunctionType

P = 128
PACK = 4
K_PASS = P * PACK
ROWS, SPLIT, H, N_OUT = 512, 384, 1024, 3072
EPS = 1.1920929e-07
MODELS = 2
PASSES = H // K_PASS
K_BLOCKS = H // P
ROW_TILES = ROWS // P
FIRST_ROW_TILE = (0, SPLIT // P)
N_ROW_TILES = (SPLIT // P, (ROWS - SPLIT) // P)
BANK = 512
CHUNK = 1024
UNITS = N_OUT // CHUNK
N_CHUNKS = MODELS * PASSES * UNITS
BANKS_PER_CHUNK = CHUNK // BANK
BASE_COLS = 624
COLS_PER_BANK = 56

FLOPS = 2 * ROWS * H * N_OUT


def tile_twomodelblockrouted_pa_kernel(tc, x, W_qkv, ln1, out):
    nc = tc.nc
    with ExitStack() as ctx:
        ctx.enter_context(tc.manual_schedule())
        consts = ctx.enter_context(tc.tile_pool(name="consts", bufs=1))
        rows_pool = ctx.enter_context(tc.tile_pool(name="rows", bufs=2))
        small = ctx.enter_context(tc.tile_pool(name="small", bufs=ROW_TILES))
        weights = ctx.enter_context(tc.tile_pool(name="weights", bufs=MODELS * PASSES))
        grouped_pool = ctx.enter_context(tc.tile_pool(name="grouped", bufs=3))
        quantised = ctx.enter_context(tc.tile_pool(name="quantised", bufs=6))
        results = ctx.enter_context(tc.tile_pool(name="results", bufs=UNITS))

        gain_rows = consts.tile([P, MODELS * H], BF16)
        nc.vector.memset(gain_rows[:].bitcast(I32), 0)
        eps = consts.tile([P, 1], F32)
        nc.vector.memset(eps[:], EPS)
        ones = consts.tile([P, P], BF16)
        nc.vector.memset(ones[:], 1.0)
        identity = consts.tile([P, P], BF16)
        make_identity(nc, identity[:])
        warm = consts.tile([P, 1], F32)
        nc.scalar.activation(out=warm[:], in_=eps[:], func=ACT.Sqrt)

        x_rows = []
        for m in range(ROW_TILES):
            x_m = rows_pool.tile([P, H], BF16, name="x_rows", bufs=ROW_TILES)
            nc.sync.dma_start(out=x_m[:], in_=x[m * P : (m + 1) * P, :])
            x_rows.append(x_m)
            if m == 0:
                nc.sync.dma_start(
                    out=gain_rows[0:1, :], in_=ln1.rearrange("(o g) k -> o (g k)", o=1)
                )
        w_raw = []
        for g in range(MODELS):
            for c in range(PASSES):
                raw = weights.tile([P, PACK, N_OUT], BF16, name="w_raw")
                nc.sync.dma_start(
                    out=raw[:],
                    in_=W_qkv[g, c * K_PASS : (c + 1) * K_PASS, :].rearrange("(t p) n -> p t n", p=P),
                )
                w_raw.append(raw)

        h_grouped = consts.tile([P, ROW_TILES, PASSES, P, PACK], BF16, align_bytes=64)
        h_codes = consts.tile([P, ROW_TILES, PASSES, P], U32, align_bytes=64)
        h_scales = consts.tile([P, ROW_TILES, PASSES, P], U8, align_bytes=64)
        with tc.psum_pool(name="head_psum", bufs=4) as head_psum:
            gains = []
            for s in range(MODELS * PASSES):
                gains_s = head_psum.tile([P, BANK], F32, name="gains")
                nc.tensor.matmul(
                    out=gains_s[:],
                    lhsT=ones[:],
                    rhs=gain_rows[:, s * BANK : (s + 1) * BANK],
                    start=True,
                    stop=True,
                )
                gains.append(gains_s)
            sum_sq = []
            h_t = []

            def sum_squares(m):
                squares = rows_pool.tile([P, H], BF16, name="squares")
                sum_sq.append(small.tile([P, 1], F32, name="sum_sq"))
                nc.scalar.activation(
                    out=squares[:], in_=x_rows[m][:], func=ACT.Square, accum_out=sum_sq[m][:]
                )

            def normalise_and_transpose(m):
                g = 0 if m < FIRST_ROW_TILE[1] else 1
                rms = small.tile([P, 1], F32, name="rms")
                nc.scalar.activation(
                    out=rms[:], in_=sum_sq[m][:], func=ACT.Sqrt, scale=1.0 / H, bias=eps[:]
                )
                rstd = small.tile([P, 1], F32, name="rstd")
                nc.vector.reciprocal(out=rstd[:], in_=rms[:])
                h_m = rows_pool.tile([P, H], BF16, name="h_rows")
                for c in range(PASSES):
                    nc.vector.scalar_tensor_tensor(
                        out=h_m[:, c * K_PASS : (c + 1) * K_PASS],
                        in0=x_rows[m][:, c * K_PASS : (c + 1) * K_PASS],
                        scalar=rstd[:],
                        in1=gains[g * PASSES + c][:],
                        op0=ALU.mult,
                        op1=ALU.mult,
                    )
                h_t.append(head_psum.tile([P, K_BLOCKS, P], BF16, name="h_t"))
                for b in range(K_BLOCKS):
                    nc.tensor.transpose(h_t[m][:, b, :], h_m[:, b * P : (b + 1) * P], identity[:])

            sum_squares(0)
            for m in range(1, ROW_TILES):
                sum_squares(m)
                normalise_and_transpose(m - 1)
            normalise_and_transpose(ROW_TILES - 1)
            for m in range(ROW_TILES):
                nc.scalar.copy(
                    out=h_grouped[:, m],
                    in_=h_t[m][:].rearrange("p (c t) r -> p c r t", t=PACK),
                )

        acc_psum = ctx.enter_context(tc.psum_pool(name="acc_psum", bufs=8))
        w_grouped = {}
        w_codes = {}
        w_scales = {}
        acc = {}

        def completes_columns(i):
            return 0 <= i < N_CHUNKS and (i // UNITS) % PASSES == PASSES - 1

        def banks_of(i):
            return BANKS_PER_CHUNK * N_ROW_TILES[i // (PASSES * UNITS)] if completes_columns(i) else 0

        def regroup(i, vector_cols):
            raw = w_raw[i // UNITS]
            first = (i % UNITS) * CHUNK
            grouped = grouped_pool.tile([P, CHUNK, PACK], BF16, name="w_grouped", align_bytes=64)
            nc.vector.tensor_copy(
                out=grouped[:, 0:vector_cols, :].rearrange("p (w i) t -> p w t i", i=4),
                in_=raw[:, :, first : first + vector_cols].rearrange("p t (w i) -> p w t i", i=4),
            )
            if vector_cols < CHUNK:
                nc.scalar.copy(
                    out=grouped[:, vector_cols:CHUNK, :].rearrange("p (w i) t -> p w t i", i=4),
                    in_=raw[:, :, first + vector_cols : first + CHUNK].rearrange(
                        "p t (w i) -> p w t i", i=4
                    ),
                )
            w_grouped[i] = grouped

        def quantise(i):
            w_codes[i] = quantised.tile([P, CHUNK], U32, name="w_codes", align_bytes=64)
            w_scales[i] = quantised.tile([P, CHUNK], U8, name="w_scales", align_bytes=64)
            nc.vector.quantize_mx(
                out=w_codes[i][:].bitcast(FP8X4),
                scales=w_scales[i][:],
                in_=w_grouped[i][:].rearrange("p w t -> p (w t)"),
            )

        def multiply(i):
            g = i // (PASSES * UNITS)
            for n in range(BANKS_PER_CHUNK):
                n_cols = slice(n * BANK, (n + 1) * BANK)
                for r in range(N_ROW_TILES[g]):
                    m = FIRST_ROW_TILE[g] + r
                    acc[(i, n, r)] = acc_psum.tile([P, BANK], F32, name="acc")
                    for c in range(PASSES):
                        chunk = i - (PASSES - 1 - c) * UNITS
                        nc.tensor.matmul_mx(
                            out=acc[(i, n, r)][:],
                            lhsT=h_codes[:, m, c, :].bitcast(FP8X4),
                            lhsT_scale=h_scales[:, m, c, :],
                            rhs=w_codes[chunk][:, n_cols].bitcast(FP8X4),
                            rhs_scale=w_scales[chunk][:, n_cols],
                            start=(c == 0),
                            stop=(c == PASSES - 1),
                        )

        def empty_and_store(i):
            g, u = i // (PASSES * UNITS), i % UNITS
            out_rows = results.tile([P, N_ROW_TILES[g], CHUNK], F32, name="out_rows%d" % g)
            for n in range(BANKS_PER_CHUNK):
                for r in range(N_ROW_TILES[g]):
                    nc.scalar.copy(
                        out=out_rows[:, r, n * BANK : (n + 1) * BANK], in_=acc[(i, n, r)][:]
                    )
            first_row = FIRST_ROW_TILE[g] * P
            nc.sync.dma_start(
                out=out[
                    first_row : first_row + N_ROW_TILES[g] * P, u * CHUNK : (u + 1) * CHUNK
                ].rearrange("(r p) n -> p r n", p=P),
                in_=out_rows[:],
            )

        for s in range(N_CHUNKS + 3):
            if s < N_CHUNKS:
                regroup(s, min(CHUNK, BASE_COLS + COLS_PER_BANK * banks_of(s - 3)))
            if s == 1:
                for m in range(ROW_TILES):
                    nc.vector.quantize_mx(
                        out=h_codes[:, m].rearrange("p c r -> p (c r)").bitcast(FP8X4),
                        scales=h_scales[:, m].rearrange("p c r -> p (c r)"),
                        in_=h_grouped[:, m].rearrange("p c r t -> p (c r t)"),
                    )
            if 0 <= s - 1 < N_CHUNKS:
                quantise(s - 1)
            if completes_columns(s - 3):
                empty_and_store(s - 3)
            if completes_columns(s - 2):
                multiply(s - 2)
